import numpy as np
import ml_dtypes


def mxq(x, axis, fmt="e4m3"):
    dtype, down = {"e4m3": (ml_dtypes.float8_e4m3fn, 7), "e5m2": (ml_dtypes.float8_e5m2, 14)}[fmt]
    v = np.moveaxis(np.asarray(x, np.float32).astype(ml_dtypes.bfloat16).astype(np.float64), axis, -1)
    blocks = v.reshape(v.shape[:-1] + (-1, 32))
    amax = np.abs(blocks).max(-1, keepdims=True)
    byte = np.maximum(np.where(amax > 0, np.frexp(amax)[1] - 1 + 127, 0) - down, 1)
    scale = np.exp2(byte - 127.0)
    codes = (blocks / scale).astype(np.float32).astype(dtype).astype(np.float64)
    return np.moveaxis((codes * scale).reshape(v.shape), -1, axis)


WIDE = False


def mx_kscale(k):
    if not WIDE:
        return np.ones(k)
    levels = np.array([10, -10, 5, -5, 0])
    a = np.random.permutation(np.resize(levels, k // 512 * 4)).reshape(k // 512, 4)
    idx = np.arange(k)
    return np.exp2(a[idx // 512, idx % 128 // 32])


BF16 = ml_dtypes.bfloat16


def bf(x):
    return np.asarray(x, np.float32).astype(BF16)


def f64(x):
    return np.asarray(x).astype(np.float64)


B, S, E, H, D = 8, 512, 512, 1, 512


def setup_inputs():
    s = mx_kscale(E)
    ckv = 0.75 * D ** 0.25 / np.sqrt(E)
    cq = 3.0 / np.sqrt(E)
    return {"x": bf(np.random.standard_normal((B, S, E)) * s),
            "Wq": bf(np.random.standard_normal((E, H * D)) * cq / s[:, None]),
            "bq": bf(np.random.standard_normal(H * D) * 0.25),
            "Wk": bf(np.random.standard_normal((E, H * D)) * ckv / s[:, None]),
            "bk": bf(np.random.standard_normal(H * D)),
            "Wv": bf(np.random.standard_normal((E, H * D)) * ckv / s[:, None]),
            "bv": bf(np.random.standard_normal(H * D))}


def reference(x, Wq, bq, Wk, bk, Wv, bv):
    xq = mxq(f64(x), 2, "e4m3")

    def proj(W, bias):
        y = (xq @ mxq(f64(W), 0, "e4m3")) + f64(bias)
        return y.reshape(B, S, H, D).transpose(0, 2, 1, 3)

    q = proj(Wq, bq)
    k = proj(Wk, bk)
    v = proj(Wv, bv)
    kv = k * np.swapaxes(v, -1, -2) * (1.0 / np.sqrt(D))
    e = np.exp(kv - kv.max(axis=2, keepdims=True))
    attn = e / e.sum(axis=2, keepdims=True)
    return np.sum(attn * q, axis=2)

@@ -1,0 +1,203 @@
+import math
+
+import concourse.mybir as mybir
+from concourse.masks import make_identity
+
+F32 = mybir.dt.float32
+BF16 = mybir.dt.bfloat16
+U32 = mybir.dt.uint32
+U8 = mybir.dt.uint8
+FP8X4 = mybir.dt.float8_e4m3fn_x4
+ALU = mybir.AluOpType
+ACT = mybir.ActivationFunctionType
+
+B = 8
+S = 512
+E = 512
+D = 512
+P = 128
+PACK = 4
+ROW_TILES = S // P
+TILES = B * ROW_TILES
+HALF = E // 2
+
+FLOPS = 2 * B * S * E * 3 * D
+
+
+def load_weight(nc, pool, w, name):
+    raw = pool.tile([P, PACK, D], BF16, name=name + "_raw")
+    nc.sync.dma_start(
+        out=raw[:].rearrange("p (u c) n -> p u (c n)", u=2),
+        in_=w.rearrange("(u p c) n -> p u (c n)", u=2, c=2),
+    )
+    return raw
+
+
+def quantise_weight(nc, pool, raw, name):
+    grouped = pool.tile([P, D, PACK], BF16, name=name + "_grouped", align_bytes=64)
+    nc.vector.tensor_copy(out=grouped[:], in_=raw[:].rearrange("p t n -> p n t"))
+    codes = pool.tile([P, D], U32, name=name + "_codes", align_bytes=64)
+    scales = pool.tile([P, D], U8, name=name + "_scales", align_bytes=64)
+    nc.vector.quantize_mx(
+        out=codes[:].bitcast(FP8X4),
+        scales=scales[:],
+        in_=grouped[:].rearrange("p n t -> p (n t)"),
+    )
+    return codes, scales
+
+
+def tile_multihead_attention_pa_t_kernel(tc, x, Wq, bq, Wk, bk, Wv, bv, out):
+    nc = tc.nc
+    inv_sqrt_d = 1.0 / math.sqrt(D)
+
+    with tc.tile_pool(name="const", bufs=1) as const, tc.tile_pool(
+        name="xin", bufs=B
+    ) as xin, tc.tile_pool(name="xq", bufs=2) as xq, tc.tile_pool(
+        name="work", bufs=4
+    ) as work, tc.psum_pool(name="ps_misc", bufs=2) as ps_misc, tc.psum_pool(
+        name="ps_proj", bufs=2
+    ) as ps_proj:
+        x_rows = []
+        for b in range(B):
+            x_sb = xin.tile([P, ROW_TILES * E], BF16, name="x_sb")
+            x_rows.append(x_sb)
+        nc.sync.dma_start(
+            out=x_rows[0][:].rearrange("p (r e) -> p r e", r=ROW_TILES),
+            in_=x[0].rearrange("(r p) e -> p r e", p=P),
+        )
+        wv_raw = load_weight(nc, const, Wv, "wv")
+        wk_raw = load_weight(nc, const, Wk, "wk")
+        wq_raw = load_weight(nc, const, Wq, "wq")
+        for b in range(1, B):
+            nc.sync.dma_start(
+                out=x_rows[b][:].rearrange("p (r e) -> p r e", r=ROW_TILES),
+                in_=x[b].rearrange("(r p) e -> p r e", p=P),
+            )
+
+        ident = const.tile([P, P], F32, name="ident")
+        make_identity(nc, ident[:])
+        ones = const.tile([P, P], BF16, name="ones")
+        nc.vector.memset(ones[:], 1.0)
+
+        bias_rows = const.tile([P, P], BF16, name="bias_rows")
+        nc.vector.memset(bias_rows[:], 0.0)
+        nc.scalar.dma_start(out=bias_rows[0:ROW_TILES, :], in_=bk.rearrange("(r c) -> r c", c=P))
+        nc.scalar.dma_start(
+            out=bias_rows[ROW_TILES : 2 * ROW_TILES, :], in_=bq.rearrange("(r c) -> r c", c=P)
+        )
+        bias_rows_f = const.tile([P, P], F32, name="bias_rows_f")
+        nc.vector.tensor_copy(out=bias_rows_f[:], in_=bias_rows[:])
+        bias_ps = ps_misc.tile([P, P], F32, tag="misc")
+        nc.tensor.transpose(bias_ps[:], bias_rows_f[:], ident[:])
+        bias_cols = const.tile([P, 2 * ROW_TILES], F32, name="bias_cols")
+        nc.vector.tensor_copy(out=bias_cols[:], in_=bias_ps[:, 0 : 2 * ROW_TILES])
+
+        bv_row = const.tile([P, D], BF16, name="bv_row")
+        nc.vector.memset(bv_row[:], 0.0)
+        nc.scalar.dma_start(out=bv_row[0:1, :], in_=bv.rearrange("(o n) -> o n", o=1))
+        bv_ps = ps_misc.tile([P, D], F32, tag="misc")
+        nc.tensor.matmul(bv_ps[:], lhsT=ones[:], rhs=bv_row[:], start=True, stop=True)
+        bv_all = const.tile([P, D], F32, name="bv_all")
+        nc.scalar.mul(out=bv_all[:], in_=bv_ps[:], mul=inv_sqrt_d)
+
+        neg_max = const.tile([P, TILES], F32, name="neg_max")
+        denom = const.tile([P, TILES], F32, name="denom")
+        numer = const.tile([P, TILES], F32, name="numer")
+        result = const.tile([P, P], F32, name="result")
+        nc.vector.memset(result[:], 0.0)
+
+        def quantise_x(b):
+            words = x_rows[b][:].bitcast(F32)
+            grouped = xq.tile([P, S * PACK], BF16, name="x_grouped", align_bytes=64)
+            grouped_words = grouped[:].bitcast(F32).rearrange(
+                "p (h r i u) -> p h r i u", h=2, r=2, u=2
+            )
+            for h in range(2):
+                xt = ps_misc.tile([P, 2, 2, P], F32, tag="misc")
+                for r in range(2):
+                    for u in range(2):
+                        first = (2 * h + r) * HALF + u * P
+                        nc.tensor.transpose(xt[:, r, u, :], words[:, first : first + P], ident[:])
+                nc.scalar.copy(out=grouped_words[:, h], in_=xt[:].rearrange("p r u i -> p r i u"))
+            codes = xq.tile([P, S], U32, name="x_codes", align_bytes=64)
+            scales = xq.tile([P, S], U8, name="x_scales", align_bytes=64)
+            nc.vector.quantize_mx(out=codes[:].bitcast(FP8X4), scales=scales[:], in_=grouped[:])
+            return codes, scales
+
+        def project(lhs_codes, lhs_scales, rhs_codes, rhs_scales, tag):
+            acc = ps_proj.tile([P, S], F32, tag=tag)
+            nc.tensor.matmul_mx(
+                out=acc[:],
+                lhsT=lhs_codes.bitcast(FP8X4),
+                lhsT_scale=lhs_scales,
+                rhs=rhs_codes.bitcast(FP8X4),
+                rhs_scale=rhs_scales,
+                start=True,
+                stop=True,
+            )
+            return acc
+
+        x_next = quantise_x(0)
+        wv_codes, wv_scales = quantise_weight(nc, const, wv_raw, "wv")
+        wk_codes, wk_scales = quantise_weight(nc, const, wk_raw, "wk")
+        wq_codes, wq_scales = quantise_weight(nc, const, wq_raw, "wq")
+
+        for b in range(B):
+            x_codes, x_scales = x_next
+            if b + 1 < B:
+                x_next = quantise_x(b + 1)
+            for jt in range(ROW_TILES):
+                t = b * ROW_TILES + jt
+                cols = slice(jt * P, (jt + 1) * P)
+                v_ps = project(x_codes[:, cols], x_scales[:, cols], wv_codes[:], wv_scales[:], "v")
+                k_ps = project(wk_codes[:, cols], wk_scales[:, cols], x_codes[:], x_scales[:], "k")
+                q_ps = project(wq_codes[:, cols], wq_scales[:, cols], x_codes[:], x_scales[:], "q")
+
+                v_sb = work.tile([P, S], F32, name="v_sb")
+                nc.scalar.mul(out=v_sb[:], in_=v_ps[:], mul=inv_sqrt_d)
+                v_biased = work.tile([P, S], F32, name="v_biased")
+                nc.gpsimd.tensor_tensor(out=v_biased[:], in0=v_sb[:], in1=bv_all[:], op=ALU.add)
+                score = work.tile([P, S], F32, name="score")
+                nc.vector.scalar_tensor_tensor(
+                    out=score[:],
+                    in0=k_ps[:],
+                    scalar=bias_cols[:, jt : jt + 1],
+                    in1=v_biased[:],
+                    op0=ALU.add,
+                    op1=ALU.mult,
+                )
+                nc.vector.tensor_reduce(
+                    out=neg_max[:, t : t + 1],
+                    in_=score[:],
+                    axis=mybir.AxisListType.X,
+                    op=ALU.max,
+                    negate=True,
+                )
+                weight = work.tile([P, S], F32, name="weight")
+                nc.scalar.activation(
+                    out=weight[:],
+                    in_=score[:],
+                    func=ACT.Exp,
+                    bias=neg_max[:, t : t + 1],
+                    scale=1.0,
+                    accum_out=denom[:, t : t + 1],
+                )
+                weighted = work.tile([P, S], F32, name="weighted")
+                nc.vector.scalar_tensor_tensor(
+                    out=weighted[:],
+                    in0=q_ps[:],
+                    scalar=bias_cols[:, ROW_TILES + jt : ROW_TILES + jt + 1],
+                    in1=weight[:],
+                    op0=ALU.add,
+                    op1=ALU.mult,
+                    accum_out=numer[:, t : t + 1],
+                )
+
+        inv_denom = const.tile([P, TILES], F32, name="inv_denom")
+        nc.vector.reciprocal(out=inv_denom[:], in_=denom[:])
+        nc.vector.tensor_mul(out=result[:, 0:TILES], in0=numer[:], in1=inv_denom[:])
+        result_ps = ps_misc.tile([P, P], F32, tag="misc")
+        nc.tensor.transpose(result_ps[:], result[:], ident[:])
+        result_rows = const.tile([TILES, P], F32, name="result_rows")
+        nc.scalar.copy(out=result_rows[:], in_=result_ps[0:TILES, :])
+        nc.sync.dma_start(out=out.rearrange("b h (r p) -> (b h r) p", p=P), in_=result_rows[:])

@@ -17,33 +17,13 @@ E = 512
 D = 512
 P = 128
 PACK = 4
-ROW_TILES = S // P
-TILES = B * ROW_TILES
-HALF = E // 2
+BLOCKS = S // P
+TILES = B * BLOCKS
+HALF_S = S // 2
+LAG_K = 2
+LAG_Q = 3
 
 FLOPS = 2 * B * S * E * 3 * D
-
-
-def load_weight(nc, pool, w, name):
-    raw = pool.tile([P, PACK, D], BF16, name=name + "_raw")
-    nc.sync.dma_start(
-        out=raw[:].rearrange("p (u c) n -> p u (c n)", u=2),
-        in_=w.rearrange("(u p c) n -> p u (c n)", u=2, c=2),
-    )
-    return raw
-
-
-def quantise_weight(nc, pool, raw, name):
-    grouped = pool.tile([P, D, PACK], BF16, name=name + "_grouped", align_bytes=64)
-    nc.vector.tensor_copy(out=grouped[:], in_=raw[:].rearrange("p t n -> p n t"))
-    codes = pool.tile([P, D], U32, name=name + "_codes", align_bytes=64)
-    scales = pool.tile([P, D], U8, name=name + "_scales", align_bytes=64)
-    nc.vector.quantize_mx(
-        out=codes[:].bitcast(FP8X4),
-        scales=scales[:],
-        in_=grouped[:].rearrange("p n t -> p (n t)"),
-    )
-    return codes, scales
 
 
 def tile_multihead_attention_pa_t_kernel(tc, x, Wq, bq, Wk, bk, Wv, bv, out):
@@ -52,80 +32,136 @@ def tile_multihead_attention_pa_t_kernel(tc, x, Wq, bq, Wk, bk, Wv, bv, out):
 
     with tc.tile_pool(name="const", bufs=1) as const, tc.tile_pool(
         name="xin", bufs=B
-    ) as xin, tc.tile_pool(name="xq", bufs=2) as xq, tc.tile_pool(
+    ) as xin, tc.tile_pool(name="xq", bufs=3) as xq, tc.tile_pool(
         name="work", bufs=4
     ) as work, tc.psum_pool(name="ps_misc", bufs=2) as ps_misc, tc.psum_pool(
         name="ps_proj", bufs=2
     ) as ps_proj:
-        x_rows = []
-        for b in range(B):
-            x_sb = xin.tile([P, ROW_TILES * E], BF16, name="x_sb")
-            x_rows.append(x_sb)
-        nc.sync.dma_start(
-            out=x_rows[0][:].rearrange("p (r e) -> p r e", r=ROW_TILES),
-            in_=x[0].rearrange("(r p) e -> p r e", p=P),
-        )
-        wv_raw = load_weight(nc, const, Wv, "wv")
-        wk_raw = load_weight(nc, const, Wk, "wk")
-        wq_raw = load_weight(nc, const, Wq, "wq")
-        for b in range(1, B):
+        bias_in = const.tile([2 * BLOCKS, P], BF16, name="bias_in")
+        nc.scalar.dma_start(out=bias_in[0:BLOCKS, :], in_=bk.rearrange("(r c) -> r c", c=P))
+        nc.scalar.dma_start(out=bias_in[BLOCKS : 2 * BLOCKS, :], in_=bq.rearrange("(r c) -> r c", c=P))
+        bv_in = const.tile([1, D], BF16, name="bv_in")
+        nc.scalar.dma_start(out=bv_in[:], in_=bv.rearrange("(o n) -> o n", o=1))
+
+        x_rows = {}
+
+        def load_x(b, h):
+            if h == 0:
+                x_rows[b] = xin.tile([P, BLOCKS * E], BF16, name="x_rows")
             nc.sync.dma_start(
-                out=x_rows[b][:].rearrange("p (r e) -> p r e", r=ROW_TILES),
-                in_=x[b].rearrange("(r p) e -> p r e", p=P),
+                out=x_rows[b][:, h * 2 * E : (h + 1) * 2 * E].rearrange("p (r e) -> p r e", r=2),
+                in_=x[b, h * HALF_S : (h + 1) * HALF_S, :].rearrange("(r p) e -> p r e", p=P),
             )
+
+        def load_weight(w, name):
+            raw = const.tile([P, PACK, D], BF16, name=name + "_raw")
+            nc.sync.dma_start(
+                out=raw[:].rearrange("p (u c) n -> p u (c n)", u=2),
+                in_=w.rearrange("(u p c) n -> p u (c n)", u=2, c=2),
+            )
+            return raw
+
+        load_x(0, 0)
+        wv_raw = load_weight(Wv, "wv")
+        load_x(0, 1)
+        wk_raw = load_weight(Wk, "wk")
+        wq_raw = load_weight(Wq, "wq")
+        for b in range(1, B):
+            load_x(b, 0)
+            load_x(b, 1)
 
         ident = const.tile([P, P], F32, name="ident")
         make_identity(nc, ident[:])
+        zero_col = const.tile([P, 1], F32, name="zero_col")
+        nc.vector.memset(zero_col[:], 0.0)
+        one_col = const.tile([P, 1], F32, name="one_col")
+        nc.scalar.activation(out=one_col[:], in_=zero_col[:], func=ACT.Exp)
         ones = const.tile([P, P], BF16, name="ones")
         nc.vector.memset(ones[:], 1.0)
-
-        bias_rows = const.tile([P, P], BF16, name="bias_rows")
+        bias_rows = const.tile([P, P], F32, name="bias_rows")
         nc.vector.memset(bias_rows[:], 0.0)
-        nc.scalar.dma_start(out=bias_rows[0:ROW_TILES, :], in_=bk.rearrange("(r c) -> r c", c=P))
-        nc.scalar.dma_start(
-            out=bias_rows[ROW_TILES : 2 * ROW_TILES, :], in_=bq.rearrange("(r c) -> r c", c=P)
-        )
-        bias_rows_f = const.tile([P, P], F32, name="bias_rows_f")
-        nc.vector.tensor_copy(out=bias_rows_f[:], in_=bias_rows[:])
-        bias_ps = ps_misc.tile([P, P], F32, tag="misc")
-        nc.tensor.transpose(bias_ps[:], bias_rows_f[:], ident[:])
-        bias_cols = const.tile([P, 2 * ROW_TILES], F32, name="bias_cols")
-        nc.vector.tensor_copy(out=bias_cols[:], in_=bias_ps[:, 0 : 2 * ROW_TILES])
-
         bv_row = const.tile([P, D], BF16, name="bv_row")
         nc.vector.memset(bv_row[:], 0.0)
-        nc.scalar.dma_start(out=bv_row[0:1, :], in_=bv.rearrange("(o n) -> o n", o=1))
-        bv_ps = ps_misc.tile([P, D], F32, tag="misc")
-        nc.tensor.matmul(bv_ps[:], lhsT=ones[:], rhs=bv_row[:], start=True, stop=True)
-        bv_all = const.tile([P, D], F32, name="bv_all")
-        nc.scalar.mul(out=bv_all[:], in_=bv_ps[:], mul=inv_sqrt_d)
-
+        result = const.tile([P, P], F32, name="result")
+        nc.vector.memset(result[:], 0.0)
         neg_max = const.tile([P, TILES], F32, name="neg_max")
         denom = const.tile([P, TILES], F32, name="denom")
         numer = const.tile([P, TILES], F32, name="numer")
-        result = const.tile([P, P], F32, name="result")
-        nc.vector.memset(result[:], 0.0)
 
-        def quantise_x(b):
+        x_grouped = {}
+        x_mx = {}
+
+        def turn_x(b, h):
+            if h == 0:
+                x_grouped[b] = xq.tile([P, S * PACK], BF16, name="x_grouped", align_bytes=64)
             words = x_rows[b][:].bitcast(F32)
-            grouped = xq.tile([P, S * PACK], BF16, name="x_grouped", align_bytes=64)
-            grouped_words = grouped[:].bitcast(F32).rearrange(
-                "p (h r i u) -> p h r i u", h=2, r=2, u=2
+            xt = ps_misc.tile([P, 2, 2, P], F32, tag="misc", name="xt")
+            for r in range(2):
+                for u in range(2):
+                    first = (2 * h + r) * (E // 2) + u * P
+                    nc.tensor.transpose(xt[:, r, u, :], words[:, first : first + P], ident[:])
+            nc.scalar.copy(
+                out=x_grouped[b][:, h * HALF_S * PACK : (h + 1) * HALF_S * PACK]
+                .bitcast(F32)
+                .rearrange("p (r i u) -> p r i u", r=2, u=2),
+                in_=xt[:].rearrange("p r u i -> p r i u"),
             )
-            for h in range(2):
-                xt = ps_misc.tile([P, 2, 2, P], F32, tag="misc")
-                for r in range(2):
-                    for u in range(2):
-                        first = (2 * h + r) * HALF + u * P
-                        nc.tensor.transpose(xt[:, r, u, :], words[:, first : first + P], ident[:])
-                nc.scalar.copy(out=grouped_words[:, h], in_=xt[:].rearrange("p r u i -> p r i u"))
-            codes = xq.tile([P, S], U32, name="x_codes", align_bytes=64)
-            scales = xq.tile([P, S], U8, name="x_scales", align_bytes=64)
-            nc.vector.quantize_mx(out=codes[:].bitcast(FP8X4), scales=scales[:], in_=grouped[:])
+
+        def quantise_x(b, h):
+            if h == 0:
+                codes = xq.tile([P, S], U32, name="x_codes", align_bytes=64)
+                scales = xq.tile([P, S], U8, name="x_scales", align_bytes=64)
+                x_mx[b] = (codes, scales)
+            codes, scales = x_mx[b]
+            half = slice(h * HALF_S, (h + 1) * HALF_S)
+            nc.vector.quantize_mx(
+                out=codes[:, half].bitcast(FP8X4),
+                scales=scales[:, half],
+                in_=x_grouped[b][:, h * HALF_S * PACK : (h + 1) * HALF_S * PACK],
+            )
+
+        def regroup_weight(raw, name):
+            grouped = const.tile([P, D, PACK], BF16, name=name + "_grouped", align_bytes=64)
+            nc.vector.tensor_copy(
+                out=grouped[:].rearrange("p (c i) t -> p c t i", i=4),
+                in_=raw[:].rearrange("p t (c i) -> p c t i", i=4),
+            )
+            return grouped
+
+        def quantise_weight(grouped, name):
+            codes = const.tile([P, D], U32, name=name + "_codes", align_bytes=64)
+            scales = const.tile([P, D], U8, name=name + "_scales", align_bytes=64)
+            nc.vector.quantize_mx(
+                out=codes[:].bitcast(FP8X4),
+                scales=scales[:],
+                in_=grouped[:].rearrange("p n t -> p (n t)"),
+            )
             return codes, scales
 
+        turn_x(0, 0)
+        nc.vector.tensor_copy(out=bias_rows[0 : 2 * BLOCKS, :], in_=bias_in[:])
+        bias_ps = ps_misc.tile([P, P], F32, tag="misc", name="bias_ps")
+        nc.tensor.transpose(bias_ps[:], bias_rows[:], ident[:])
+        bias_cols = const.tile([P, 2 * BLOCKS], F32, name="bias_cols")
+        nc.vector.tensor_copy(out=bias_cols[:], in_=bias_ps[:, 0 : 2 * BLOCKS])
+        nc.vector.tensor_copy(out=bv_row[0:1, :], in_=bv_in[:])
+        bv_ps = ps_misc.tile([P, D], F32, tag="misc", name="bv_ps")
+        nc.tensor.matmul(bv_ps[:], lhsT=ones[:], rhs=bv_row[:], start=True, stop=True)
+        bv_all = const.tile([P, D], F32, name="bv_all")
+        nc.scalar.mul(out=bv_all[:], in_=bv_ps[:], mul=inv_sqrt_d)
+        turn_x(0, 1)
+
+        wv_grouped = regroup_weight(wv_raw, "wv")
+        quantise_x(0, 0)
+        wv_codes, wv_scales = quantise_weight(wv_grouped, "wv")
+        quantise_x(0, 1)
+        wk_grouped = regroup_weight(wk_raw, "wk")
+        wk_codes, wk_scales = quantise_weight(wk_grouped, "wk")
+        wq_grouped = regroup_weight(wq_raw, "wq")
+        wq_codes, wq_scales = quantise_weight(wq_grouped, "wq")
+
         def project(lhs_codes, lhs_scales, rhs_codes, rhs_scales, tag):
-            acc = ps_proj.tile([P, S], F32, tag=tag)
+            acc = ps_proj.tile([P, S], F32, tag=tag, name=tag + "_ps")
             nc.tensor.matmul_mx(
                 out=acc[:],
                 lhsT=lhs_codes.bitcast(FP8X4),
@@ -137,66 +173,82 @@ def tile_multihead_attention_pa_t_kernel(tc, x, Wq, bq, Wk, bk, Wv, bv, out):
             )
             return acc
 
-        x_next = quantise_x(0)
-        wv_codes, wv_scales = quantise_weight(nc, const, wv_raw, "wv")
-        wk_codes, wk_scales = quantise_weight(nc, const, wk_raw, "wk")
-        wq_codes, wq_scales = quantise_weight(nc, const, wq_raw, "wq")
+        v_biased = {}
+        weight = {}
 
-        for b in range(B):
-            x_codes, x_scales = x_next
-            if b + 1 < B:
-                x_next = quantise_x(b + 1)
-            for jt in range(ROW_TILES):
-                t = b * ROW_TILES + jt
-                cols = slice(jt * P, (jt + 1) * P)
-                v_ps = project(x_codes[:, cols], x_scales[:, cols], wv_codes[:], wv_scales[:], "v")
-                k_ps = project(wk_codes[:, cols], wk_scales[:, cols], x_codes[:], x_scales[:], "k")
-                q_ps = project(wq_codes[:, cols], wq_scales[:, cols], x_codes[:], x_scales[:], "q")
+        def stage_v(t):
+            x_codes, x_scales = x_mx[t // BLOCKS]
+            cols = slice((t % BLOCKS) * P, (t % BLOCKS + 1) * P)
+            v_ps = project(x_codes[:, cols], x_scales[:, cols], wv_codes[:], wv_scales[:], "v")
+            v_sb = work.tile([P, S], F32, name="v_sb")
+            nc.scalar.mul(out=v_sb[:], in_=v_ps[:], mul=inv_sqrt_d)
+            v_biased[t] = work.tile([P, S], F32, name="v_biased")
+            nc.gpsimd.tensor_tensor(out=v_biased[t][:], in0=v_sb[:], in1=bv_all[:], op=ALU.add)
 
-                v_sb = work.tile([P, S], F32, name="v_sb")
-                nc.scalar.mul(out=v_sb[:], in_=v_ps[:], mul=inv_sqrt_d)
-                v_biased = work.tile([P, S], F32, name="v_biased")
-                nc.gpsimd.tensor_tensor(out=v_biased[:], in0=v_sb[:], in1=bv_all[:], op=ALU.add)
-                score = work.tile([P, S], F32, name="score")
-                nc.vector.scalar_tensor_tensor(
-                    out=score[:],
-                    in0=k_ps[:],
-                    scalar=bias_cols[:, jt : jt + 1],
-                    in1=v_biased[:],
-                    op0=ALU.add,
-                    op1=ALU.mult,
-                )
-                nc.vector.tensor_reduce(
-                    out=neg_max[:, t : t + 1],
-                    in_=score[:],
-                    axis=mybir.AxisListType.X,
-                    op=ALU.max,
-                    negate=True,
-                )
-                weight = work.tile([P, S], F32, name="weight")
-                nc.scalar.activation(
-                    out=weight[:],
-                    in_=score[:],
-                    func=ACT.Exp,
-                    bias=neg_max[:, t : t + 1],
-                    scale=1.0,
-                    accum_out=denom[:, t : t + 1],
-                )
-                weighted = work.tile([P, S], F32, name="weighted")
-                nc.vector.scalar_tensor_tensor(
-                    out=weighted[:],
-                    in0=q_ps[:],
-                    scalar=bias_cols[:, ROW_TILES + jt : ROW_TILES + jt + 1],
-                    in1=weight[:],
-                    op0=ALU.add,
-                    op1=ALU.mult,
-                    accum_out=numer[:, t : t + 1],
-                )
+        def stage_k(t):
+            x_codes, x_scales = x_mx[t // BLOCKS]
+            jt = t % BLOCKS
+            cols = slice(jt * P, (jt + 1) * P)
+            k_ps = project(wk_codes[:, cols], wk_scales[:, cols], x_codes[:], x_scales[:], "k")
+            score = work.tile([P, S], F32, name="score")
+            nc.vector.scalar_tensor_tensor(
+                out=score[:],
+                in0=k_ps[:],
+                scalar=bias_cols[:, jt : jt + 1],
+                in1=v_biased[t][:],
+                op0=ALU.add,
+                op1=ALU.mult,
+            )
+            nc.vector.tensor_reduce(
+                out=neg_max[:, t : t + 1],
+                in_=score[:],
+                axis=mybir.AxisListType.X,
+                op=ALU.max,
+                negate=True,
+            )
+            weight[t] = work.tile([P, S], F32, name="weight")
+            nc.scalar.activation(
+                out=weight[t][:],
+                in_=score[:],
+                func=ACT.Exp,
+                bias=neg_max[:, t : t + 1],
+                scale=1.0,
+                accum_out=denom[:, t : t + 1],
+            )
+
+        def stage_q(t):
+            x_codes, x_scales = x_mx[t // BLOCKS]
+            jt = t % BLOCKS
+            cols = slice(jt * P, (jt + 1) * P)
+            q_ps = project(wq_codes[:, cols], wq_scales[:, cols], x_codes[:], x_scales[:], "q")
+            weighted = work.tile([P, S], F32, name="weighted")
+            nc.vector.scalar_tensor_tensor(
+                out=weighted[:],
+                in0=q_ps[:],
+                scalar=bias_cols[:, BLOCKS + jt : BLOCKS + jt + 1],
+                in1=weight[t][:],
+                op0=ALU.add,
+                op1=ALU.mult,
+                accum_out=numer[:, t : t + 1],
+            )
+
+        for step in range(TILES + LAG_Q):
+            if step < TILES:
+                stage_v(step)
+            if LAG_K <= step < TILES + LAG_K:
+                stage_k(step - LAG_K)
+            if LAG_Q <= step:
+                stage_q(step - LAG_Q)
+            if step % BLOCKS == 1 and step // BLOCKS + 1 < B:
+                turn_x(step // BLOCKS + 1, 0)
+                turn_x(step // BLOCKS + 1, 1)
+                quantise_x(step // BLOCKS + 1, 0)
+                quantise_x(step // BLOCKS + 1, 1)
 
         inv_denom = const.tile([P, TILES], F32, name="inv_denom")
         nc.vector.reciprocal(out=inv_denom[:], in_=denom[:])
         nc.vector.tensor_mul(out=result[:, 0:TILES], in0=numer[:], in1=inv_denom[:])
-        result_ps = ps_misc.tile([P, P], F32, tag="misc")
+        result_ps = ps_misc.tile([P, P], F32, tag="misc", name="result_ps")
         nc.tensor.transpose(result_ps[:], result[:], ident[:])
         result_rows = const.tile([TILES, P], F32, name="result_rows")
         nc.scalar.copy(out=result_rows[:], in_=result_ps[0:TILES, :])

@@ -20,8 +20,9 @@ PACK = 4
 BLOCKS = S // P
 TILES = B * BLOCKS
 HALF_S = S // 2
-LAG_K = 2
-LAG_Q = 3
+LAG_K = 1
+LAG_SCORE = 2
+LAG_Q = 4
 
 FLOPS = 2 * B * S * E * 3 * D
 
@@ -36,7 +37,7 @@ def tile_multihead_attention_pa_t_kernel(tc, x, Wq, bq, Wk, bk, Wv, bv, out):
         name="work", bufs=4
     ) as work, tc.psum_pool(name="ps_misc", bufs=2) as ps_misc, tc.psum_pool(
         name="ps_proj", bufs=2
-    ) as ps_proj:
+    ) as ps_proj, tc.manual_schedule():
         bias_in = const.tile([2 * BLOCKS, P], BF16, name="bias_in")
         nc.scalar.dma_start(out=bias_in[0:BLOCKS, :], in_=bk.rearrange("(r c) -> r c", c=P))
         nc.scalar.dma_start(out=bias_in[BLOCKS : 2 * BLOCKS, :], in_=bq.rearrange("(r c) -> r c", c=P))
@@ -107,36 +108,31 @@ def tile_multihead_attention_pa_t_kernel(tc, x, Wq, bq, Wk, bk, Wv, bv, out):
                 in_=xt[:].rearrange("p r u i -> p r i u"),
             )
 
-        def quantise_x(b, h):
-            if h == 0:
-                codes = xq.tile([P, S], U32, name="x_codes", align_bytes=64)
-                scales = xq.tile([P, S], U8, name="x_scales", align_bytes=64)
-                x_mx[b] = (codes, scales)
-            codes, scales = x_mx[b]
-            half = slice(h * HALF_S, (h + 1) * HALF_S)
-            nc.vector.quantize_mx(
-                out=codes[:, half].bitcast(FP8X4),
-                scales=scales[:, half],
-                in_=x_grouped[b][:, h * HALF_S * PACK : (h + 1) * HALF_S * PACK],
-            )
+        def quantise_x(b):
+            codes = xq.tile([P, S], U32, name="x_codes", align_bytes=64)
+            scales = xq.tile([P, S], U8, name="x_scales", align_bytes=64)
+            nc.vector.quantize_mx(out=codes[:].bitcast(FP8X4), scales=scales[:], in_=x_grouped[b][:])
+            x_mx[b] = (codes, scales)
+
+        w_grouped = {}
+        w_mx = {}
 
         def regroup_weight(raw, name):
-            grouped = const.tile([P, D, PACK], BF16, name=name + "_grouped", align_bytes=64)
+            w_grouped[name] = const.tile([P, D, PACK], BF16, name=name + "_grouped", align_bytes=64)
             nc.vector.tensor_copy(
-                out=grouped[:].rearrange("p (c i) t -> p c t i", i=4),
+                out=w_grouped[name][:].rearrange("p (c i) t -> p c t i", i=4),
                 in_=raw[:].rearrange("p t (c i) -> p c t i", i=4),
             )
-            return grouped
 
-        def quantise_weight(grouped, name):
+        def quantise_weight(name):
             codes = const.tile([P, D], U32, name=name + "_codes", align_bytes=64)
             scales = const.tile([P, D], U8, name=name + "_scales", align_bytes=64)
             nc.vector.quantize_mx(
                 out=codes[:].bitcast(FP8X4),
                 scales=scales[:],
-                in_=grouped[:].rearrange("p n t -> p (n t)"),
+                in_=w_grouped[name][:].rearrange("p n t -> p (n t)"),
             )
-            return codes, scales
+            w_mx[name] = (codes, scales)
 
         turn_x(0, 0)
         nc.vector.tensor_copy(out=bias_rows[0 : 2 * BLOCKS, :], in_=bias_in[:])
@@ -151,57 +147,58 @@ def tile_multihead_attention_pa_t_kernel(tc, x, Wq, bq, Wk, bk, Wv, bv, out):
         nc.scalar.mul(out=bv_all[:], in_=bv_ps[:], mul=inv_sqrt_d)
         turn_x(0, 1)
 
-        wv_grouped = regroup_weight(wv_raw, "wv")
-        quantise_x(0, 0)
-        wv_codes, wv_scales = quantise_weight(wv_grouped, "wv")
-        quantise_x(0, 1)
-        wk_grouped = regroup_weight(wk_raw, "wk")
-        wk_codes, wk_scales = quantise_weight(wk_grouped, "wk")
-        wq_grouped = regroup_weight(wq_raw, "wq")
-        wq_codes, wq_scales = quantise_weight(wq_grouped, "wq")
+        regroup_weight(wv_raw, "wv")
+        quantise_weight("wv")
+        quantise_x(0)
+        regroup_weight(wk_raw, "wk")
+        quantise_weight("wk")
 
-        def project(lhs_codes, lhs_scales, rhs_codes, rhs_scales, tag):
+        def project(lhs, lhs_cols, rhs, tag):
             acc = ps_proj.tile([P, S], F32, tag=tag, name=tag + "_ps")
             nc.tensor.matmul_mx(
                 out=acc[:],
-                lhsT=lhs_codes.bitcast(FP8X4),
-                lhsT_scale=lhs_scales,
-                rhs=rhs_codes.bitcast(FP8X4),
-                rhs_scale=rhs_scales,
+                lhsT=lhs[0][:, lhs_cols].bitcast(FP8X4),
+                lhsT_scale=lhs[1][:, lhs_cols],
+                rhs=rhs[0][:].bitcast(FP8X4),
+                rhs_scale=rhs[1][:],
                 start=True,
                 stop=True,
             )
             return acc
 
+        def block_cols(t):
+            return slice((t % BLOCKS) * P, (t % BLOCKS + 1) * P)
+
         v_biased = {}
+        k_ps = {}
+        score = {}
         weight = {}
 
         def stage_v(t):
-            x_codes, x_scales = x_mx[t // BLOCKS]
-            cols = slice((t % BLOCKS) * P, (t % BLOCKS + 1) * P)
-            v_ps = project(x_codes[:, cols], x_scales[:, cols], wv_codes[:], wv_scales[:], "v")
+            v_ps = project(x_mx[t // BLOCKS], block_cols(t), w_mx["wv"], "v")
             v_sb = work.tile([P, S], F32, name="v_sb")
             nc.scalar.mul(out=v_sb[:], in_=v_ps[:], mul=inv_sqrt_d)
             v_biased[t] = work.tile([P, S], F32, name="v_biased")
             nc.gpsimd.tensor_tensor(out=v_biased[t][:], in0=v_sb[:], in1=bv_all[:], op=ALU.add)
 
         def stage_k(t):
-            x_codes, x_scales = x_mx[t // BLOCKS]
-            jt = t % BLOCKS
-            cols = slice(jt * P, (jt + 1) * P)
-            k_ps = project(wk_codes[:, cols], wk_scales[:, cols], x_codes[:], x_scales[:], "k")
-            score = work.tile([P, S], F32, name="score")
+            k_ps[t] = project(w_mx["wk"], block_cols(t), x_mx[t // BLOCKS], "k")
+
+        def stage_score(t):
+            score[t] = work.tile([P, S], F32, name="score")
             nc.vector.scalar_tensor_tensor(
-                out=score[:],
-                in0=k_ps[:],
-                scalar=bias_cols[:, jt : jt + 1],
+                out=score[t][:],
+                in0=k_ps[t][:],
+                scalar=bias_cols[:, t % BLOCKS : t % BLOCKS + 1],
                 in1=v_biased[t][:],
                 op0=ALU.add,
                 op1=ALU.mult,
             )
+
+        def stage_softmax(t):
             nc.vector.tensor_reduce(
                 out=neg_max[:, t : t + 1],
-                in_=score[:],
+                in_=score[t][:],
                 axis=mybir.AxisListType.X,
                 op=ALU.max,
                 negate=True,
@@ -209,7 +206,7 @@ def tile_multihead_attention_pa_t_kernel(tc, x, Wq, bq, Wk, bk, Wv, bv, out):
             weight[t] = work.tile([P, S], F32, name="weight")
             nc.scalar.activation(
                 out=weight[t][:],
-                in_=score[:],
+                in_=score[t][:],
                 func=ACT.Exp,
                 bias=neg_max[:, t : t + 1],
                 scale=1.0,
@@ -217,15 +214,12 @@ def tile_multihead_attention_pa_t_kernel(tc, x, Wq, bq, Wk, bk, Wv, bv, out):
             )
 
         def stage_q(t):
-            x_codes, x_scales = x_mx[t // BLOCKS]
-            jt = t % BLOCKS
-            cols = slice(jt * P, (jt + 1) * P)
-            q_ps = project(wq_codes[:, cols], wq_scales[:, cols], x_codes[:], x_scales[:], "q")
+            q_ps = project(w_mx["wq"], block_cols(t), x_mx[t // BLOCKS], "q")
             weighted = work.tile([P, S], F32, name="weighted")
             nc.vector.scalar_tensor_tensor(
                 out=weighted[:],
                 in0=q_ps[:],
-                scalar=bias_cols[:, BLOCKS + jt : BLOCKS + jt + 1],
+                scalar=bias_cols[:, BLOCKS + t % BLOCKS : BLOCKS + t % BLOCKS + 1],
                 in1=weight[t][:],
                 op0=ALU.add,
                 op1=ALU.mult,
@@ -235,15 +229,23 @@ def tile_multihead_attention_pa_t_kernel(tc, x, Wq, bq, Wk, bk, Wv, bv, out):
         for step in range(TILES + LAG_Q):
             if step < TILES:
                 stage_v(step)
-            if LAG_K <= step < TILES + LAG_K:
+            if 0 <= step - LAG_K < TILES:
                 stage_k(step - LAG_K)
-            if LAG_Q <= step:
+            if 0 <= step - LAG_SCORE < TILES:
+                stage_score(step - LAG_SCORE)
+            if 0 <= step - LAG_Q:
                 stage_q(step - LAG_Q)
-            if step % BLOCKS == 1 and step // BLOCKS + 1 < B:
-                turn_x(step // BLOCKS + 1, 0)
-                turn_x(step // BLOCKS + 1, 1)
-                quantise_x(step // BLOCKS + 1, 0)
-                quantise_x(step // BLOCKS + 1, 1)
+            if step == LAG_Q - 2:
+                regroup_weight(wq_raw, "wq")
+            if step == LAG_Q - 1:
+                quantise_weight("wq")
+            if 0 <= step - LAG_SCORE < TILES:
+                stage_softmax(step - LAG_SCORE)
+            next_b = step // BLOCKS + 1
+            if next_b < B and step % BLOCKS < 2:
+                turn_x(next_b, step % BLOCKS)
+            if next_b < B and step % BLOCKS == 2:
+                quantise_x(next_b)
 
         inv_denom = const.tile([P, TILES], F32, name="inv_denom")
         nc.vector.reciprocal(out=inv_denom[:], in_=denom[:])

import math

import concourse.mybir as mybir
from concourse.masks import make_identity

F32 = mybir.dt.float32
BF16 = mybir.dt.bfloat16
U32 = mybir.dt.uint32
U8 = mybir.dt.uint8
FP8X4 = mybir.dt.float8_e4m3fn_x4
ALU = mybir.AluOpType
ACT = mybir.ActivationFunctionType

B = 8
S = 512
E = 512
D = 512
P = 128
PACK = 4
BLOCKS = S // P
TILES = B * BLOCKS
HALF_S = S // 2
LAG_K = 1
LAG_SCORE = 2
LAG_Q = 4

FLOPS = 2 * B * S * E * 3 * D


def tile_multihead_attention_pa_t_kernel(tc, x, Wq, bq, Wk, bk, Wv, bv, out):
    nc = tc.nc
    inv_sqrt_d = 1.0 / math.sqrt(D)

    with tc.tile_pool(name="const", bufs=1) as const, tc.tile_pool(
        name="xin", bufs=B
    ) as xin, tc.tile_pool(name="xq", bufs=3) as xq, tc.tile_pool(
        name="work", bufs=4
    ) as work, tc.psum_pool(name="ps_misc", bufs=2) as ps_misc, tc.psum_pool(
        name="ps_proj", bufs=2
    ) as ps_proj, tc.manual_schedule():
        bias_in = const.tile([2 * BLOCKS, P], BF16, name="bias_in")
        nc.scalar.dma_start(out=bias_in[0:BLOCKS, :], in_=bk.rearrange("(r c) -> r c", c=P))
        nc.scalar.dma_start(out=bias_in[BLOCKS : 2 * BLOCKS, :], in_=bq.rearrange("(r c) -> r c", c=P))
        bv_in = const.tile([1, D], BF16, name="bv_in")
        nc.scalar.dma_start(out=bv_in[:], in_=bv.rearrange("(o n) -> o n", o=1))

        x_rows = {}

        def load_x(b, h):
            if h == 0:
                x_rows[b] = xin.tile([P, BLOCKS * E], BF16, name="x_rows")
            nc.sync.dma_start(
                out=x_rows[b][:, h * 2 * E : (h + 1) * 2 * E].rearrange("p (r e) -> p r e", r=2),
                in_=x[b, h * HALF_S : (h + 1) * HALF_S, :].rearrange("(r p) e -> p r e", p=P),
            )

        def load_weight(w, name):
            raw = const.tile([P, PACK, D], BF16, name=name + "_raw")
            nc.sync.dma_start(
                out=raw[:].rearrange("p (u c) n -> p u (c n)", u=2),
                in_=w.rearrange("(u p c) n -> p u (c n)", u=2, c=2),
            )
            return raw

        load_x(0, 0)
        wv_raw = load_weight(Wv, "wv")
        load_x(0, 1)
        wk_raw = load_weight(Wk, "wk")
        wq_raw = load_weight(Wq, "wq")
        for b in range(1, B):
            load_x(b, 0)
            load_x(b, 1)

        ident = const.tile([P, P], F32, name="ident")
        make_identity(nc, ident[:])
        zero_col = const.tile([P, 1], F32, name="zero_col")
        nc.vector.memset(zero_col[:], 0.0)
        one_col = const.tile([P, 1], F32, name="one_col")
        nc.scalar.activation(out=one_col[:], in_=zero_col[:], func=ACT.Exp)
        ones = const.tile([P, P], BF16, name="ones")
        nc.vector.memset(ones[:], 1.0)
        bias_rows = const.tile([P, P], F32, name="bias_rows")
        nc.vector.memset(bias_rows[:], 0.0)
        bv_row = const.tile([P, D], BF16, name="bv_row")
        nc.vector.memset(bv_row[:], 0.0)
        result = const.tile([P, P], F32, name="result")
        nc.vector.memset(result[:], 0.0)
        neg_max = const.tile([P, TILES], F32, name="neg_max")
        denom = const.tile([P, TILES], F32, name="denom")
        numer = const.tile([P, TILES], F32, name="numer")

        x_grouped = {}
        x_mx = {}

        def turn_x(b, h):
            if h == 0:
                x_grouped[b] = xq.tile([P, S * PACK], BF16, name="x_grouped", align_bytes=64)
            words = x_rows[b][:].bitcast(F32)
            xt = ps_misc.tile([P, 2, 2, P], F32, tag="misc", name="xt")
            for r in range(2):
                for u in range(2):
                    first = (2 * h + r) * (E // 2) + u * P
                    nc.tensor.transpose(xt[:, r, u, :], words[:, first : first + P], ident[:])
            nc.scalar.copy(
                out=x_grouped[b][:, h * HALF_S * PACK : (h + 1) * HALF_S * PACK]
                .bitcast(F32)
                .rearrange("p (r i u) -> p r i u", r=2, u=2),
                in_=xt[:].rearrange("p r u i -> p r i u"),
            )

        def quantise_x(b):
            codes = xq.tile([P, S], U32, name="x_codes", align_bytes=64)
            scales = xq.tile([P, S], U8, name="x_scales", align_bytes=64)
            nc.vector.quantize_mx(out=codes[:].bitcast(FP8X4), scales=scales[:], in_=x_grouped[b][:])
            x_mx[b] = (codes, scales)

        w_grouped = {}
        w_mx = {}

        def regroup_weight(raw, name):
            w_grouped[name] = const.tile([P, D, PACK], BF16, name=name + "_grouped", align_bytes=64)
            nc.vector.tensor_copy(
                out=w_grouped[name][:].rearrange("p (c i) t -> p c t i", i=4),
                in_=raw[:].rearrange("p t (c i) -> p c t i", i=4),
            )

        def quantise_weight(name):
            codes = const.tile([P, D], U32, name=name + "_codes", align_bytes=64)
            scales = const.tile([P, D], U8, name=name + "_scales", align_bytes=64)
            nc.vector.quantize_mx(
                out=codes[:].bitcast(FP8X4),
                scales=scales[:],
                in_=w_grouped[name][:].rearrange("p n t -> p (n t)"),
            )
            w_mx[name] = (codes, scales)

        turn_x(0, 0)
        nc.vector.tensor_copy(out=bias_rows[0 : 2 * BLOCKS, :], in_=bias_in[:])
        bias_ps = ps_misc.tile([P, P], F32, tag="misc", name="bias_ps")
        nc.tensor.transpose(bias_ps[:], bias_rows[:], ident[:])
        bias_cols = const.tile([P, 2 * BLOCKS], F32, name="bias_cols")
        nc.vector.tensor_copy(out=bias_cols[:], in_=bias_ps[:, 0 : 2 * BLOCKS])
        nc.vector.tensor_copy(out=bv_row[0:1, :], in_=bv_in[:])
        bv_ps = ps_misc.tile([P, D], F32, tag="misc", name="bv_ps")
        nc.tensor.matmul(bv_ps[:], lhsT=ones[:], rhs=bv_row[:], start=True, stop=True)
        bv_all = const.tile([P, D], F32, name="bv_all")
        nc.scalar.mul(out=bv_all[:], in_=bv_ps[:], mul=inv_sqrt_d)
        turn_x(0, 1)

        regroup_weight(wv_raw, "wv")
        quantise_weight("wv")
        quantise_x(0)
        regroup_weight(wk_raw, "wk")
        quantise_weight("wk")

        def project(lhs, lhs_cols, rhs, tag):
            acc = ps_proj.tile([P, S], F32, tag=tag, name=tag + "_ps")
            nc.tensor.matmul_mx(
                out=acc[:],
                lhsT=lhs[0][:, lhs_cols].bitcast(FP8X4),
                lhsT_scale=lhs[1][:, lhs_cols],
                rhs=rhs[0][:].bitcast(FP8X4),
                rhs_scale=rhs[1][:],
                start=True,
                stop=True,
            )
            return acc

        def block_cols(t):
            return slice((t % BLOCKS) * P, (t % BLOCKS + 1) * P)

        v_biased = {}
        k_ps = {}
        score = {}
        weight = {}

        def stage_v(t):
            v_ps = project(x_mx[t // BLOCKS], block_cols(t), w_mx["wv"], "v")
            v_sb = work.tile([P, S], F32, name="v_sb")
            nc.scalar.mul(out=v_sb[:], in_=v_ps[:], mul=inv_sqrt_d)
            v_biased[t] = work.tile([P, S], F32, name="v_biased")
            nc.gpsimd.tensor_tensor(out=v_biased[t][:], in0=v_sb[:], in1=bv_all[:], op=ALU.add)

        def stage_k(t):
            k_ps[t] = project(w_mx["wk"], block_cols(t), x_mx[t // BLOCKS], "k")

        def stage_score(t):
            score[t] = work.tile([P, S], F32, name="score")
            nc.vector.scalar_tensor_tensor(
                out=score[t][:],
                in0=k_ps[t][:],
                scalar=bias_cols[:, t % BLOCKS : t % BLOCKS + 1],
                in1=v_biased[t][:],
                op0=ALU.add,
                op1=ALU.mult,
            )

        def stage_softmax(t):
            nc.vector.tensor_reduce(
                out=neg_max[:, t : t + 1],
                in_=score[t][:],
                axis=mybir.AxisListType.X,
                op=ALU.max,
                negate=True,
            )
            weight[t] = work.tile([P, S], F32, name="weight")
            nc.scalar.activation(
                out=weight[t][:],
                in_=score[t][:],
                func=ACT.Exp,
                bias=neg_max[:, t : t + 1],
                scale=1.0,
                accum_out=denom[:, t : t + 1],
            )

        def stage_q(t):
            q_ps = project(w_mx["wq"], block_cols(t), x_mx[t // BLOCKS], "q")
            weighted = work.tile([P, S], F32, name="weighted")
            nc.vector.scalar_tensor_tensor(
                out=weighted[:],
                in0=q_ps[:],
                scalar=bias_cols[:, BLOCKS + t % BLOCKS : BLOCKS + t % BLOCKS + 1],
                in1=weight[t][:],
                op0=ALU.add,
                op1=ALU.mult,
                accum_out=numer[:, t : t + 1],
            )

        for step in range(TILES + LAG_Q):
            if step < TILES:
                stage_v(step)
            if 0 <= step - LAG_K < TILES:
                stage_k(step - LAG_K)
            if 0 <= step - LAG_SCORE < TILES:
                stage_score(step - LAG_SCORE)
            if 0 <= step - LAG_Q:
                stage_q(step - LAG_Q)
            if step == LAG_Q - 2:
                regroup_weight(wq_raw, "wq")
            if step == LAG_Q - 1:
                quantise_weight("wq")
            if 0 <= step - LAG_SCORE < TILES:
                stage_softmax(step - LAG_SCORE)
            next_b = step // BLOCKS + 1
            if next_b < B and step % BLOCKS < 2:
                turn_x(next_b, step % BLOCKS)
            if next_b < B and step % BLOCKS == 2:
                quantise_x(next_b)

        inv_denom = const.tile([P, TILES], F32, name="inv_denom")
        nc.vector.reciprocal(out=inv_denom[:], in_=denom[:])
        nc.vector.tensor_mul(out=result[:, 0:TILES], in0=numer[:], in1=inv_denom[:])
        result_ps = ps_misc.tile([P, P], F32, tag="misc", name="result_ps")
        nc.tensor.transpose(result_ps[:], result[:], ident[:])
        result_rows = const.tile([TILES, P], F32, name="result_rows")
        nc.scalar.copy(out=result_rows[:], in_=result_ps[0:TILES, :])
        nc.sync.dma_start(out=out.rearrange("b h (r p) -> (b h r) p", p=P), in_=result_rows[:])
